import numpy as np
import ml_dtypes

BF16 = ml_dtypes.bfloat16


def bf(x):
    return np.asarray(x, np.float32).astype(BF16)


def f32(x):
    return np.asarray(x, np.float32)


def f64(x):
    return np.asarray(x).astype(np.float64)


def striped(idx):
    return np.tile(idx.reshape(-1, 16).T, (8, 1))


K, D, S, N = 256, 256, 512, 256


def setup_inputs():
    base = f32(np.random.uniform(1.0, 8.0, (K, S)))
    z = bf(np.random.standard_normal((D, N)) * (0.5 + np.random.random((1, N))) * np.sqrt(2.0 / D))
    cent = bf(np.random.standard_normal((D, K)) * (0.5 + np.random.random((1, K))) * np.sqrt(2.0 / D))
    return {"base": base, "z": z, "cent": cent, "offs": striped(np.random.permutation(S)[:N])}


def reference(base, z, cent, offs):
    idx = offs[:16].T.reshape(-1)
    zz = f64(z)
    cc = f64(cent)
    z2 = (zz * zz).sum(axis=0)[None, :]
    c2 = (cc * cc).sum(axis=0)[:, None]
    cross = cc.T @ zz
    out = f64(base).copy()
    out[:, idx] = (z2 + c2) + (-2.0 * cross)
    return out

@@ -1,0 +1,58 @@
+import concourse.mybir as mybir
+
+P = 128
+K, D, S, N = 256, 256, 512, 256
+KB = K // P
+DB = D // P
+
+FLOPS = 2 * K * N * D + 2 * D * (K + N)
+
+BF16, F32, U16 = mybir.dt.bfloat16, mybir.dt.float32, mybir.dt.uint16
+ADD, MULT = mybir.AluOpType.add, mybir.AluOpType.mult
+COPY = mybir.ActivationFunctionType.Copy
+
+
+def tile_dtcclusterlayer_kernel(tc, base, z, cent, offs, out):
+    nc = tc.nc
+    with (
+        tc.tile_pool(name="held", bufs=1) as held,
+        tc.psum_pool(name="psum", bufs=1) as psum,
+    ):
+        offsets = held.tile([P, N // 16], U16, name="offsets")
+        nc.sync.dma_start(offsets[:], offs)
+        z_sb = held.tile([P, DB, N], BF16, name="z_sb")
+        nc.sync.dma_start(z_sb[:], z.rearrange("(b p) j -> p b j", p=P))
+        cent_sb = held.tile([P, DB, K], BF16, name="cent_sb")
+        nc.scalar.dma_start(cent_sb[:], cent.rearrange("(b p) k -> p b k", p=P))
+        windows = [held.tile([P, S], F32, name=f"window{kb}") for kb in range(KB)]
+        for kb in range(KB):
+            nc.gpsimd.dma_start(windows[kb][:], base[kb * P : (kb + 1) * P, :])
+
+        ones = held.tile([P, N], BF16, name="ones")
+        nc.gpsimd.memset(ones[:], 1.0)
+        z_sq = held.tile([P, DB, N], BF16, name="z_sq")
+        nc.vector.tensor_tensor(z_sq[:], z_sb[:], z_sb[:], MULT)
+        cent_sq = held.tile([P, DB, K], BF16, name="cent_sq")
+        nc.gpsimd.tensor_tensor(cent_sq[:], cent_sb[:], cent_sb[:], MULT)
+
+        for kb in range(KB):
+            block = slice(kb * P, (kb + 1) * P)
+
+            cross = psum.tile([P, N], F32, name=f"cross{kb}")
+            for db in range(DB):
+                nc.tensor.matmul(
+                    cross[:], cent_sb[:, db, block], z_sb[:, db, :], start=(db == 0), stop=(db == DB - 1)
+                )
+            neg = held.tile([P, N], F32, name=f"neg{kb}")
+            nc.scalar.activation(neg[:], cross[:], COPY, scale=-2.0)
+
+            sums = psum.tile([P, N], F32, name=f"sums{kb}")
+            for db in range(DB):
+                nc.tensor.matmul(sums[:], ones[:, :P], z_sq[:, db, :], start=(db == 0), stop=False)
+            for db in range(DB):
+                nc.tensor.matmul(sums[:], cent_sq[:, db, block], ones[:], start=False, stop=(db == DB - 1))
+            nrm = held.tile([P, N], F32, name=f"nrm{kb}")
+            nc.scalar.activation(nrm[:], sums[:], COPY)
+
+            nc.vector.tensor_tensor(windows[kb][:].indirect(offsets[:]), nrm[:], neg[:], ADD)
+            nc.sync.dma_start(out[block, :], windows[kb][:])

@@ -14,45 +14,48 @@ COPY = mybir.ActivationFunctionType.Copy
 
 def tile_dtcclusterlayer_kernel(tc, base, z, cent, offs, out):
     nc = tc.nc
+    queues = [nc.sync, nc.scalar]
+    blocks = [slice(kb * P, (kb + 1) * P) for kb in range(KB)]
     with (
         tc.tile_pool(name="held", bufs=1) as held,
         tc.psum_pool(name="psum", bufs=1) as psum,
     ):
-        offsets = held.tile([P, N // 16], U16, name="offsets")
-        nc.sync.dma_start(offsets[:], offs)
         z_sb = held.tile([P, DB, N], BF16, name="z_sb")
         nc.sync.dma_start(z_sb[:], z.rearrange("(b p) j -> p b j", p=P))
         cent_sb = held.tile([P, DB, K], BF16, name="cent_sb")
         nc.scalar.dma_start(cent_sb[:], cent.rearrange("(b p) k -> p b k", p=P))
+        offsets = held.tile([P, N // 16], U16, name="offsets")
+        nc.sync.dma_start(offsets[:], offs)
         windows = [held.tile([P, S], F32, name=f"window{kb}") for kb in range(KB)]
         for kb in range(KB):
-            nc.gpsimd.dma_start(windows[kb][:], base[kb * P : (kb + 1) * P, :])
+            queues[kb].dma_start(windows[kb][:], base[blocks[kb], :])
 
         ones = held.tile([P, N], BF16, name="ones")
-        nc.gpsimd.memset(ones[:], 1.0)
+        nc.vector.memset(ones[:], 1.0)
         z_sq = held.tile([P, DB, N], BF16, name="z_sq")
         nc.vector.tensor_tensor(z_sq[:], z_sb[:], z_sb[:], MULT)
         cent_sq = held.tile([P, DB, K], BF16, name="cent_sq")
-        nc.gpsimd.tensor_tensor(cent_sq[:], cent_sb[:], cent_sb[:], MULT)
+        nc.vector.tensor_tensor(cent_sq[:], cent_sb[:], cent_sb[:], MULT)
 
+        negs = []
         for kb in range(KB):
-            block = slice(kb * P, (kb + 1) * P)
-
             cross = psum.tile([P, N], F32, name=f"cross{kb}")
             for db in range(DB):
                 nc.tensor.matmul(
-                    cross[:], cent_sb[:, db, block], z_sb[:, db, :], start=(db == 0), stop=(db == DB - 1)
+                    cross[:], cent_sb[:, db, blocks[kb]], z_sb[:, db, :], start=(db == 0), stop=(db == DB - 1)
                 )
             neg = held.tile([P, N], F32, name=f"neg{kb}")
             nc.scalar.activation(neg[:], cross[:], COPY, scale=-2.0)
+            negs.append(neg)
 
+        for kb in range(KB):
             sums = psum.tile([P, N], F32, name=f"sums{kb}")
             for db in range(DB):
                 nc.tensor.matmul(sums[:], ones[:, :P], z_sq[:, db, :], start=(db == 0), stop=False)
             for db in range(DB):
-                nc.tensor.matmul(sums[:], cent_sq[:, db, block], ones[:], start=False, stop=(db == DB - 1))
+                nc.tensor.matmul(sums[:], cent_sq[:, db, blocks[kb]], ones[:], start=False, stop=(db == DB - 1))
             nrm = held.tile([P, N], F32, name=f"nrm{kb}")
             nc.scalar.activation(nrm[:], sums[:], COPY)
 
-            nc.vector.tensor_tensor(windows[kb][:].indirect(offsets[:]), nrm[:], neg[:], ADD)
-            nc.sync.dma_start(out[block, :], windows[kb][:])
+            nc.vector.tensor_tensor(windows[kb][:].indirect(offsets[:]), nrm[:], negs[kb][:], ADD)
+            queues[kb].dma_start(out[blocks[kb], :], windows[kb][:])

@@ -15,7 +15,6 @@ COPY = mybir.ActivationFunctionType.Copy
 def tile_dtcclusterlayer_kernel(tc, base, z, cent, offs, out):
     nc = tc.nc
     queues = [nc.sync, nc.scalar]
-    blocks = [slice(kb * P, (kb + 1) * P) for kb in range(KB)]
     with (
         tc.tile_pool(name="held", bufs=1) as held,
         tc.psum_pool(name="psum", bufs=1) as psum,
@@ -28,34 +27,34 @@ def tile_dtcclusterlayer_kernel(tc, base, z, cent, offs, out):
         nc.sync.dma_start(offsets[:], offs)
         windows = [held.tile([P, S], F32, name=f"window{kb}") for kb in range(KB)]
         for kb in range(KB):
-            queues[kb].dma_start(windows[kb][:], base[blocks[kb], :])
+            queues[kb].dma_start(windows[kb][:], base[kb * P : (kb + 1) * P, :])
 
         ones = held.tile([P, N], BF16, name="ones")
         nc.vector.memset(ones[:], 1.0)
+
         z_sq = held.tile([P, DB, N], BF16, name="z_sq")
         nc.vector.tensor_tensor(z_sq[:], z_sb[:], z_sb[:], MULT)
         cent_sq = held.tile([P, DB, K], BF16, name="cent_sq")
         nc.vector.tensor_tensor(cent_sq[:], cent_sb[:], cent_sb[:], MULT)
 
-        negs = []
         for kb in range(KB):
+            block = slice(kb * P, (kb + 1) * P)
+
             cross = psum.tile([P, N], F32, name=f"cross{kb}")
             for db in range(DB):
                 nc.tensor.matmul(
-                    cross[:], cent_sb[:, db, blocks[kb]], z_sb[:, db, :], start=(db == 0), stop=(db == DB - 1)
+                    cross[:], cent_sb[:, db, block], z_sb[:, db, :], start=(db == 0), stop=(db == DB - 1)
                 )
             neg = held.tile([P, N], F32, name=f"neg{kb}")
             nc.scalar.activation(neg[:], cross[:], COPY, scale=-2.0)
-            negs.append(neg)
 
-        for kb in range(KB):
             sums = psum.tile([P, N], F32, name=f"sums{kb}")
             for db in range(DB):
                 nc.tensor.matmul(sums[:], ones[:, :P], z_sq[:, db, :], start=(db == 0), stop=False)
             for db in range(DB):
-                nc.tensor.matmul(sums[:], cent_sq[:, db, blocks[kb]], ones[:], start=False, stop=(db == DB - 1))
+                nc.tensor.matmul(sums[:], cent_sq[:, db, block], ones[:], start=False, stop=(db == DB - 1))
             nrm = held.tile([P, N], F32, name=f"nrm{kb}")
             nc.scalar.activation(nrm[:], sums[:], COPY)
 
-            nc.vector.tensor_tensor(windows[kb][:].indirect(offsets[:]), nrm[:], negs[kb][:], ADD)
-            queues[kb].dma_start(out[blocks[kb], :], windows[kb][:])
+            nc.vector.tensor_tensor(windows[kb][:].indirect(offsets[:]), nrm[:], neg[:], ADD)
+            queues[kb].dma_start(out[block, :], windows[kb][:])

@@ -15,36 +15,35 @@ COPY = mybir.ActivationFunctionType.Copy
 def tile_dtcclusterlayer_kernel(tc, base, z, cent, offs, out):
     nc = tc.nc
     queues = [nc.sync, nc.scalar]
+    blocks = [slice(kb * P, (kb + 1) * P) for kb in range(KB)]
     with (
         tc.tile_pool(name="held", bufs=1) as held,
         tc.psum_pool(name="psum", bufs=1) as psum,
     ):
         z_sb = held.tile([P, DB, N], BF16, name="z_sb")
         nc.sync.dma_start(z_sb[:], z.rearrange("(b p) j -> p b j", p=P))
-        cent_sb = held.tile([P, DB, K], BF16, name="cent_sb")
-        nc.scalar.dma_start(cent_sb[:], cent.rearrange("(b p) k -> p b k", p=P))
+        cent_sb = [held.tile([P, DB, P], BF16, name=f"cent_sb{kb}") for kb in range(KB)]
+        for kb in range(KB):
+            nc.scalar.dma_start(cent_sb[kb][:], cent[:, blocks[kb]].rearrange("(b p) k -> p b k", p=P))
         offsets = held.tile([P, N // 16], U16, name="offsets")
         nc.sync.dma_start(offsets[:], offs)
         windows = [held.tile([P, S], F32, name=f"window{kb}") for kb in range(KB)]
         for kb in range(KB):
-            queues[kb].dma_start(windows[kb][:], base[kb * P : (kb + 1) * P, :])
+            queues[kb].dma_start(windows[kb][:], base[blocks[kb], :])
 
         ones = held.tile([P, N], BF16, name="ones")
         nc.vector.memset(ones[:], 1.0)
 
         z_sq = held.tile([P, DB, N], BF16, name="z_sq")
         nc.vector.tensor_tensor(z_sq[:], z_sb[:], z_sb[:], MULT)
-        cent_sq = held.tile([P, DB, K], BF16, name="cent_sq")
-        nc.vector.tensor_tensor(cent_sq[:], cent_sb[:], cent_sb[:], MULT)
 
         for kb in range(KB):
-            block = slice(kb * P, (kb + 1) * P)
+            cent_sq = held.tile([P, DB, P], BF16, name=f"cent_sq{kb}")
+            nc.vector.tensor_tensor(cent_sq[:], cent_sb[kb][:], cent_sb[kb][:], MULT)
 
             cross = psum.tile([P, N], F32, name=f"cross{kb}")
             for db in range(DB):
-                nc.tensor.matmul(
-                    cross[:], cent_sb[:, db, block], z_sb[:, db, :], start=(db == 0), stop=(db == DB - 1)
-                )
+                nc.tensor.matmul(cross[:], cent_sb[kb][:, db, :], z_sb[:, db, :], start=(db == 0), stop=(db == DB - 1))
             neg = held.tile([P, N], F32, name=f"neg{kb}")
             nc.scalar.activation(neg[:], cross[:], COPY, scale=-2.0)
 
@@ -52,9 +51,9 @@ def tile_dtcclusterlayer_kernel(tc, base, z, cent, offs, out):
             for db in range(DB):
                 nc.tensor.matmul(sums[:], ones[:, :P], z_sq[:, db, :], start=(db == 0), stop=False)
             for db in range(DB):
-                nc.tensor.matmul(sums[:], cent_sq[:, db, block], ones[:], start=False, stop=(db == DB - 1))
+                nc.tensor.matmul(sums[:], cent_sq[:, db, :], ones[:], start=False, stop=(db == DB - 1))
             nrm = held.tile([P, N], F32, name=f"nrm{kb}")
             nc.scalar.activation(nrm[:], sums[:], COPY)
 
             nc.vector.tensor_tensor(windows[kb][:].indirect(offsets[:]), nrm[:], neg[:], ADD)
-            queues[kb].dma_start(out[block, :], windows[kb][:])
+            queues[kb].dma_start(out[blocks[kb], :], windows[kb][:])

@@ -5,6 +5,8 @@ K, D, S, N = 256, 256, 512, 256
 KB = K // P
 DB = D // P
 
+WARM_MATMULS = 6
+
 FLOPS = 2 * K * N * D + 2 * D * (K + N)
 
 BF16, F32, U16 = mybir.dt.bfloat16, mybir.dt.float32, mybir.dt.uint16
@@ -33,6 +35,10 @@ def tile_dtcclusterlayer_kernel(tc, base, z, cent, offs, out):
 
         ones = held.tile([P, N], BF16, name="ones")
         nc.vector.memset(ones[:], 1.0)
+
+        warm = psum.tile([P, N], F32, name="warm")
+        for i in range(WARM_MATMULS):
+            nc.tensor.matmul(warm[:], ones[:, :P], ones[:], start=True, stop=True)
 
         z_sq = held.tile([P, DB, N], BF16, name="z_sq")
         nc.vector.tensor_tensor(z_sq[:], z_sb[:], z_sb[:], MULT)

@@ -11,7 +11,7 @@ FLOPS = 2 * K * N * D + 2 * D * (K + N)
 
 BF16, F32, U16 = mybir.dt.bfloat16, mybir.dt.float32, mybir.dt.uint16
 ADD, MULT = mybir.AluOpType.add, mybir.AluOpType.mult
-COPY = mybir.ActivationFunctionType.Copy
+COPY, IDENTITY = mybir.ActivationFunctionType.Copy, mybir.ActivationFunctionType.Identity
 
 
 def tile_dtcclusterlayer_kernel(tc, base, z, cent, offs, out):
@@ -43,6 +43,8 @@ def tile_dtcclusterlayer_kernel(tc, base, z, cent, offs, out):
         z_sq = held.tile([P, DB, N], BF16, name="z_sq")
         nc.vector.tensor_tensor(z_sq[:], z_sb[:], z_sb[:], MULT)
 
+        z2 = psum.tile([P, N], F32, name="z2")
+
         for kb in range(KB):
             cent_sq = held.tile([P, DB, P], BF16, name=f"cent_sq{kb}")
             nc.vector.tensor_tensor(cent_sq[:], cent_sb[kb][:], cent_sb[kb][:], MULT)
@@ -53,13 +55,20 @@ def tile_dtcclusterlayer_kernel(tc, base, z, cent, offs, out):
             neg = held.tile([P, N], F32, name=f"neg{kb}")
             nc.scalar.activation(neg[:], cross[:], COPY, scale=-2.0)
 
-            sums = psum.tile([P, N], F32, name=f"sums{kb}")
+            if kb == 0:
+                for db in range(DB):
+                    nc.tensor.matmul(z2[:], ones[:, :P], z_sq[:, db, :], start=(db == 0), stop=(db == DB - 1))
+            c2 = psum.tile([P, 1], F32, name=f"c2_{kb}")
             for db in range(DB):
-                nc.tensor.matmul(sums[:], ones[:, :P], z_sq[:, db, :], start=(db == 0), stop=False)
-            for db in range(DB):
-                nc.tensor.matmul(sums[:], cent_sq[:, db, :], ones[:], start=False, stop=(db == DB - 1))
+                nc.tensor.matmul(c2[:], cent_sq[:, db, :], ones[:, :1], start=(db == 0), stop=(db == DB - 1))
+
             nrm = held.tile([P, N], F32, name=f"nrm{kb}")
-            nc.scalar.activation(nrm[:], sums[:], COPY)
+            if kb == 0:
+                nc.vector.tensor_scalar(nrm[:], z2[:], c2[:], None, ADD)
+            else:
+                c2_sb = held.tile([P, 1], F32, name="c2_sb")
+                nc.scalar.activation(c2_sb[:], c2[:], COPY)
+                nc.scalar.activation(nrm[:], z2[:], IDENTITY, bias=c2_sb[:])
 
             nc.vector.tensor_tensor(windows[kb][:].indirect(offsets[:]), nrm[:], neg[:], ADD)
             queues[kb].dma_start(out[blocks[kb], :], windows[kb][:])

@@ -53,7 +53,10 @@ def tile_dtcclusterlayer_kernel(tc, base, z, cent, offs, out):
             for db in range(DB):
                 nc.tensor.matmul(cross[:], cent_sb[kb][:, db, :], z_sb[:, db, :], start=(db == 0), stop=(db == DB - 1))
             neg = held.tile([P, N], F32, name=f"neg{kb}")
-            nc.scalar.activation(neg[:], cross[:], COPY, scale=-2.0)
+            if kb == 0:
+                nc.vector.tensor_scalar(neg[:], cross[:], -2.0, None, MULT)
+            else:
+                nc.scalar.activation(neg[:], cross[:], COPY, scale=-2.0)
 
             if kb == 0:
                 for db in range(DB):

@@ -11,7 +11,11 @@ FLOPS = 2 * K * N * D + 2 * D * (K + N)
 
 BF16, F32, U16 = mybir.dt.bfloat16, mybir.dt.float32, mybir.dt.uint16
 ADD, MULT = mybir.AluOpType.add, mybir.AluOpType.mult
-COPY, IDENTITY = mybir.ActivationFunctionType.Copy, mybir.ActivationFunctionType.Identity
+COPY, IDENTITY, SQUARE = (
+    mybir.ActivationFunctionType.Copy,
+    mybir.ActivationFunctionType.Identity,
+    mybir.ActivationFunctionType.Square,
+)
 
 
 def tile_dtcclusterlayer_kernel(tc, base, z, cent, offs, out):
@@ -47,7 +51,10 @@ def tile_dtcclusterlayer_kernel(tc, base, z, cent, offs, out):
 
         for kb in range(KB):
             cent_sq = held.tile([P, DB, P], BF16, name=f"cent_sq{kb}")
-            nc.vector.tensor_tensor(cent_sq[:], cent_sb[kb][:], cent_sb[kb][:], MULT)
+            if kb == 0:
+                nc.vector.tensor_tensor(cent_sq[:], cent_sb[kb][:], cent_sb[kb][:], MULT)
+            else:
+                nc.scalar.activation(cent_sq[:], cent_sb[kb][:], SQUARE)
 
             cross = psum.tile([P, N], F32, name=f"cross{kb}")
             for db in range(DB):

@@ -44,8 +44,9 @@ def tile_dtcclusterlayer_kernel(tc, base, z, cent, offs, out):
         for i in range(WARM_MATMULS):
             nc.tensor.matmul(warm[:], ones[:, :P], ones[:], start=True, stop=True)
 
-        z_sq = held.tile([P, DB, N], BF16, name="z_sq")
-        nc.vector.tensor_tensor(z_sq[:], z_sb[:], z_sb[:], MULT)
+        z_sq = [held.tile([P, N], BF16, name=f"z_sq{db}") for db in range(DB)]
+        for db in range(DB):
+            nc.vector.tensor_tensor(z_sq[db][:], z_sb[:, db, :], z_sb[:, db, :], MULT)
 
         z2 = psum.tile([P, N], F32, name="z2")
 
@@ -67,7 +68,7 @@ def tile_dtcclusterlayer_kernel(tc, base, z, cent, offs, out):
 
             if kb == 0:
                 for db in range(DB):
-                    nc.tensor.matmul(z2[:], ones[:, :P], z_sq[:, db, :], start=(db == 0), stop=(db == DB - 1))
+                    nc.tensor.matmul(z2[:], ones[:, :P], z_sq[db][:], start=(db == 0), stop=(db == DB - 1))
             c2 = psum.tile([P, 1], F32, name=f"c2_{kb}")
             for db in range(DB):
                 nc.tensor.matmul(c2[:], cent_sq[:, db, :], ones[:, :1], start=(db == 0), stop=(db == DB - 1))

import concourse.mybir as mybir

P = 128
K, D, S, N = 256, 256, 512, 256
KB = K // P
DB = D // P

WARM_MATMULS = 6

FLOPS = 2 * K * N * D + 2 * D * (K + N)

BF16, F32, U16 = mybir.dt.bfloat16, mybir.dt.float32, mybir.dt.uint16
ADD, MULT = mybir.AluOpType.add, mybir.AluOpType.mult
COPY, IDENTITY, SQUARE = (
    mybir.ActivationFunctionType.Copy,
    mybir.ActivationFunctionType.Identity,
    mybir.ActivationFunctionType.Square,
)


def tile_dtcclusterlayer_kernel(tc, base, z, cent, offs, out):
    nc = tc.nc
    queues = [nc.sync, nc.scalar]
    blocks = [slice(kb * P, (kb + 1) * P) for kb in range(KB)]
    with (
        tc.tile_pool(name="held", bufs=1) as held,
        tc.psum_pool(name="psum", bufs=1) as psum,
    ):
        z_sb = held.tile([P, DB, N], BF16, name="z_sb")
        nc.sync.dma_start(z_sb[:], z.rearrange("(b p) j -> p b j", p=P))
        cent_sb = [held.tile([P, DB, P], BF16, name=f"cent_sb{kb}") for kb in range(KB)]
        for kb in range(KB):
            nc.scalar.dma_start(cent_sb[kb][:], cent[:, blocks[kb]].rearrange("(b p) k -> p b k", p=P))
        offsets = held.tile([P, N // 16], U16, name="offsets")
        nc.sync.dma_start(offsets[:], offs)
        windows = [held.tile([P, S], F32, name=f"window{kb}") for kb in range(KB)]
        for kb in range(KB):
            queues[kb].dma_start(windows[kb][:], base[blocks[kb], :])

        ones = held.tile([P, N], BF16, name="ones")
        nc.vector.memset(ones[:], 1.0)

        warm = psum.tile([P, N], F32, name="warm")
        for i in range(WARM_MATMULS):
            nc.tensor.matmul(warm[:], ones[:, :P], ones[:], start=True, stop=True)

        z_sq = [held.tile([P, N], BF16, name=f"z_sq{db}") for db in range(DB)]
        for db in range(DB):
            nc.vector.tensor_tensor(z_sq[db][:], z_sb[:, db, :], z_sb[:, db, :], MULT)

        z2 = psum.tile([P, N], F32, name="z2")

        for kb in range(KB):
            cent_sq = held.tile([P, DB, P], BF16, name=f"cent_sq{kb}")
            if kb == 0:
                nc.vector.tensor_tensor(cent_sq[:], cent_sb[kb][:], cent_sb[kb][:], MULT)
            else:
                nc.scalar.activation(cent_sq[:], cent_sb[kb][:], SQUARE)

            cross = psum.tile([P, N], F32, name=f"cross{kb}")
            for db in range(DB):
                nc.tensor.matmul(cross[:], cent_sb[kb][:, db, :], z_sb[:, db, :], start=(db == 0), stop=(db == DB - 1))
            neg = held.tile([P, N], F32, name=f"neg{kb}")
            if kb == 0:
                nc.vector.tensor_scalar(neg[:], cross[:], -2.0, None, MULT)
            else:
                nc.scalar.activation(neg[:], cross[:], COPY, scale=-2.0)

            if kb == 0:
                for db in range(DB):
                    nc.tensor.matmul(z2[:], ones[:, :P], z_sq[db][:], start=(db == 0), stop=(db == DB - 1))
            c2 = psum.tile([P, 1], F32, name=f"c2_{kb}")
            for db in range(DB):
                nc.tensor.matmul(c2[:], cent_sq[:, db, :], ones[:, :1], start=(db == 0), stop=(db == DB - 1))

            nrm = held.tile([P, N], F32, name=f"nrm{kb}")
            if kb == 0:
                nc.vector.tensor_scalar(nrm[:], z2[:], c2[:], None, ADD)
            else:
                c2_sb = held.tile([P, 1], F32, name="c2_sb")
                nc.scalar.activation(c2_sb[:], c2[:], COPY)
                nc.scalar.activation(nrm[:], z2[:], IDENTITY, bias=c2_sb[:])

            nc.vector.tensor_tensor(windows[kb][:].indirect(offsets[:]), nrm[:], neg[:], ADD)
            queues[kb].dma_start(out[blocks[kb], :], windows[kb][:])
